import numpy as np
import ml_dtypes


def mxq(x, axis, fmt="e4m3"):
    dtype, down = {"e4m3": (ml_dtypes.float8_e4m3fn, 7), "e5m2": (ml_dtypes.float8_e5m2, 14)}[fmt]
    v = np.moveaxis(np.asarray(x, np.float32).astype(ml_dtypes.bfloat16).astype(np.float64), axis, -1)
    blocks = v.reshape(v.shape[:-1] + (-1, 32))
    amax = np.abs(blocks).max(-1, keepdims=True)
    byte = np.maximum(np.where(amax > 0, np.frexp(amax)[1] - 1 + 127, 0) - down, 1)
    scale = np.exp2(byte - 127.0)
    codes = (blocks / scale).astype(np.float32).astype(dtype).astype(np.float64)
    return np.moveaxis((codes * scale).reshape(v.shape), -1, axis)


WIDE = False


def mx_kscale(k):
    if not WIDE:
        return np.ones(k)
    levels = np.array([10, -10, 5, -5, 0])
    if k % 512:
        return np.exp2(np.random.permutation(np.resize(levels, k // 32))).repeat(32)
    a = np.empty((k // 512, 16))
    for p in range(k // 512):
        a[p, :8] = np.random.permutation(np.resize(levels, 8))
        for g in range(8):
            far = levels[np.abs(levels - a[p, g]) >= 10]
            a[p, g + 8] = far[np.random.randint(len(far))]
    return np.exp2(a.ravel()).repeat(32)


BF16 = ml_dtypes.bfloat16


def bf(x):
    return np.asarray(x, np.float32).astype(BF16)


def f64(x):
    return np.asarray(x).astype(np.float64)


B, D_IN, D_H = 512, 1024, 1024


def sigmoid(v):
    return 1.0 / (1.0 + np.exp(-v))


def setup_inputs():
    s = mx_kscale(B)[:, None]
    u = mx_kscale(D_H)

    def w_in():
        return bf(np.random.standard_normal((D_H, D_IN)) * 0.6 / np.sqrt(D_IN))

    def w_rec():
        return bf(np.random.standard_normal((D_H, D_H)) * 0.6 / np.sqrt(D_H))

    def bias():
        return bf(np.random.standard_normal(D_H) * 0.3)

    x0 = bf(np.random.standard_normal((B, D_IN)))
    h = bf(np.random.standard_normal((B, D_H)))
    W_i0 = w_in()
    b_W_i = bias()
    W_c0 = w_in()
    b_W_c = bias()
    U_i = w_rec()
    b_U_i = bias()
    U_c = w_rec()
    b_U_c = bias()
    g = bf(np.random.standard_normal((B, D_H)) * np.exp2(np.random.randint(-6, 1, (B, 1))) * 4.0 / s * u[None, :])
    I_gate = sigmoid(f64(x0) @ f64(W_i0).T + f64(b_W_i) + f64(h) @ f64(U_i).T + f64(b_U_i))
    C_head = f64(x0) @ f64(W_c0).T + f64(b_W_c) + f64(h) @ f64(U_c).T + f64(b_U_c)
    return {"incoming": bf(f64(x0) * s), "h": h,
            "W_i": bf(f64(W_i0) / u[:, None]), "b_W_i": b_W_i,
            "W_c": bf(f64(W_c0) / u[:, None]), "b_W_c": b_W_c,
            "U_i": U_i, "b_U_i": b_U_i, "U_c": U_c, "b_U_c": b_U_c,
            "I_gate": np.asarray(I_gate, np.float32), "C_head": np.asarray(C_head, np.float32),
            "grad_out": g}


def reference(incoming, h, W_i, b_W_i, W_c, b_W_c, U_i, b_U_i, U_c, b_U_c, I_gate, C_head, grad_out):
    g = f64(grad_out)
    ig = f64(I_gate)
    ch = f64(C_head)
    dzi = g * ch * ig * (1.0 - ig)
    dc = g * ig
    a = mxq(dzi, 1, "e5m2") @ mxq(f64(W_i), 0, "e4m3")
    c = mxq(dc, 1, "e5m2") @ mxq(f64(W_c), 0, "e4m3")
    dx = a + c
    dw = mxq(dzi, 0, "e5m2").T @ mxq(f64(incoming), 0, "e4m3")
    return dx, dw

@@ -1,0 +1,359 @@
+from contextlib import ExitStack
+
+import concourse.mybir as mybir
+from concourse.masks import make_identity
+
+B, D_IN, D_H = 512, 1024, 1024
+FLOPS = 2 * B * D_H * D_IN * 3
+BYTES = 2 * B * D_IN + 2 * 2 * D_H * D_IN + 2 * 4 * B * D_H + 2 * B * D_H + 4 * B * D_IN + 4 * D_H * D_IN
+
+F32 = mybir.dt.float32
+BF16 = mybir.dt.bfloat16
+U32 = mybir.dt.uint32
+U8 = mybir.dt.uint8
+E4 = mybir.dt.float8_e4m3fn_x4
+E5 = mybir.dt.float8_e5m2_x4
+MULT = mybir.AluOpType.mult
+SUB = mybir.AluOpType.subtract
+
+P = 128
+PACK = 4
+HALF = 512
+
+
+def tile_lstmcell_pa_v_kernel(
+    tc, incoming, h, W_i, b_W_i, W_c, b_W_c, U_i, b_U_i, U_c, b_U_c, I_gate, C_head, grad_out, out_0, out_1
+):
+    nc = tc.nc
+    with ExitStack() as ctx:
+        raw = ctx.enter_context(tc.tile_pool(name="raw", bufs=1))
+        keep = ctx.enter_context(tc.tile_pool(name="keep", bufs=1))
+        rot = ctx.enter_context(tc.tile_pool(name="rot", bufs=2))
+        psum = ctx.enter_context(tc.psum_pool(name="psum", bufs=8))
+        ctx.enter_context(tc.manual_schedule())
+
+        g_v = grad_out.rearrange("(p j) w -> p j w", j=PACK)
+        ig_v = I_gate.rearrange("(p j) w -> p j w", j=PACK)
+        ch_v = C_head.rearrange("(p j) w -> p j w", j=PACK)
+        inc_v = incoming.rearrange("(p j) n -> p j n", j=PACK)
+        w_v = [
+            W_i.rearrange("(g p j) n -> p g j n", g=2, j=PACK),
+            W_c.rearrange("(g p j) n -> p g j n", g=2, j=PACK),
+        ]
+        o0_v = out_0.rearrange("(p j) n -> p j n", j=PACK)
+
+        def load(view, shape, dtype, name):
+            t = raw.tile(shape, dtype, name=name)
+            nc.sync.dma_start(out=t[:], in_=view)
+            return t
+
+        g_u = {}
+        ig_u = {}
+        ch_u = {}
+        v_u = {}
+        dcf_u = {}
+        dcf_j = {}
+        src = {}
+        il = {}
+        dest = {}
+        codes = {}
+        tps = {}
+        fqs = {}
+        accs = {}
+        outs = {}
+
+        def new_codes(name):
+            c = keep.tile([P, HALF], U32, name="c%s" % name, align_bytes=64)
+            s = keep.tile([P, HALF], U8, name="s%s" % name, align_bytes=64)
+            codes[name] = (c, s)
+
+        def L_ga(hf, j0, nj):
+            ws = slice(HALF * hf, HALF * (hf + 1))
+            g_u[(hf, j0)] = load(g_v[:, j0 : j0 + nj, ws], [P, nj, HALF], BF16, "g%d%d" % (hf, j0))
+            ig_u[(hf, j0)] = load(ig_v[:, j0 : j0 + nj, ws], [P, nj, HALF], F32, "ig%d%d" % (hf, j0))
+
+        def L_ch(hf, j0, nj):
+            ws = slice(HALF * hf, HALF * (hf + 1))
+            ch_u[(hf, j0)] = load(ch_v[:, j0 : j0 + nj, ws], [P, nj, HALF], F32, "ch%d%d" % (hf, j0))
+
+        def L_i(u, hn, n0, nn):
+            t = load(inc_v[:, :, HALF * hn + n0 : HALF * hn + n0 + nn], [P, PACK, nn], BF16, u)
+            src[u] = t[:]
+            if codes.get("i%d" % hn) is None:
+                new_codes("i%d" % hn)
+            dest[u] = ("i%d" % hn, n0, nn)
+
+        def L_w(x, g):
+            t = load(w_v[x][:, g, :, :], [P, PACK, D_IN], BF16, "w%d%d" % (x, g))
+            for hn in range(2):
+                u = "w%d%d%d" % (x, g, hn)
+                src[u] = t[:, :, HALF * hn : HALF * (hn + 1)]
+                new_codes(u)
+                dest[u] = (u, 0, HALF)
+
+        dzi_h = [keep.tile([P, PACK, HALF], BF16, name="dzi%d" % hf, align_bytes=64) for hf in range(2)]
+        for hf in range(2):
+            src["t%d" % hf] = dzi_h[hf][:]
+            new_codes("t%d" % hf)
+            dest["t%d" % hf] = ("t%d" % hf, 0, HALF)
+
+        def copy(engine, out, in_):
+            if engine == "V":
+                nc.vector.tensor_copy(out=out, in_=in_)
+            else:
+                nc.scalar.copy(out=out, in_=in_)
+
+        def IL(u, engine):
+            nn = dest[u][2]
+            t = rot.tile([P, nn, PACK], BF16, name="il", tag="il", bufs=8, align_bytes=64)
+            copy(engine, t[:], src[u].rearrange("p j n -> p n j"))
+            il[u] = t[:].rearrange("p n j -> p (n j)")
+
+        def Q(u):
+            name, n0, nn = dest[u]
+            fmt = E4 if u[0] in "iw" else E5
+            c, s = codes[name]
+            nc.vector.quantize_mx(out=c[:, n0 : n0 + nn].bitcast(fmt), scales=s[:, n0 : n0 + nn], in_=il[u])
+
+        def EA(hf, j0):
+            k = (hf, j0)
+            nj = g_u[k].shape[1]
+            dcf = keep.tile([P, nj, HALF], F32, name="dcf%d%d" % k)
+            nc.vector.tensor_tensor(out=dcf[:], in0=g_u[k][:], in1=ig_u[k][:], op=MULT)
+            dcf_u[k] = dcf
+            for jj in range(nj):
+                dcf_j[(hf, j0 + jj)] = dcf[:, jj, :]
+
+        def EB(hf, j0):
+            k = (hf, j0)
+            nj = g_u[k].shape[1]
+            v = rot.tile([P, nj, HALF], F32, name="v", tag="v", bufs=2)
+            nc.vector.scalar_tensor_tensor(out=v[:], in0=ig_u[k][:], scalar=1.0, in1=ch_u[k][:], op0=SUB, op1=MULT)
+            v_u[k] = v
+
+        def EC(hf, j0):
+            k = (hf, j0)
+            nj = g_u[k].shape[1]
+            nc.vector.scalar_tensor_tensor(
+                out=dzi_h[hf][:, j0 : j0 + nj, :], in0=v_u[k][:], scalar=-1.0, in1=dcf_u[k][:], op0=MULT, op1=MULT
+            )
+
+        def T(hf, jp):
+            k = (hf, jp)
+            tz = psum.tile([P, 2, 2, P], F32, name="bank", tag="bank")
+            for jj in range(2):
+                words = dzi_h[hf][:, 2 * jp + jj, :].bitcast(F32)
+                for u in range(2):
+                    nc.tensor.transpose(tz[:, jj, u, :], words[:, u : HALF // 2 : 2], ident[:])
+            banks = [tz]
+            for jj in range(2):
+                tcx = psum.tile([P, PACK, P], F32, name="bank", tag="bank")
+                for t in range(PACK):
+                    nc.tensor.transpose(tcx[:, t, :], dcf_j[(hf, 2 * jp + jj)][:, t:HALF:PACK], ident[:])
+                banks.append(tcx)
+            tps[k] = banks
+            f = keep.tile([P, 2, 2, P, PACK], BF16, name="fq%d%d" % k, align_bytes=64)
+            fqs[k] = f
+            u = "f%d%d" % k
+            il[u] = f[:].rearrange("p x j r t -> p (x j r t)")
+            new_codes(u)
+            dest[u] = (u, 0, HALF)
+
+        def EvT(hf, jp, i, engine):
+            k = (hf, jp)
+            f = fqs[k]
+            if i == 0:
+                copy(engine, f[:, 0, :, :, :].bitcast(F32), tps[k][0][:].rearrange("p j u r -> p j r u"))
+            else:
+                copy(engine, f[:, 1, i - 1, :, :], tps[k][i][:].rearrange("p t r -> p r t"))
+
+        def MM1(m):
+            hf, mm = divmod(m, 4)
+            cols = slice(P * mm, P * (mm + 1))
+            c, s = codes["t%d" % hf]
+            for hn in range(2):
+                acc = psum.tile([P, HALF], F32, name="bank", tag="bank")
+                ci, si = codes["i%d" % hn]
+                nc.tensor.matmul_mx(
+                    out=acc[:],
+                    lhsT=c[:, cols].bitcast(E5),
+                    lhsT_scale=s[:, cols],
+                    rhs=ci[:].bitcast(E4),
+                    rhs_scale=si[:],
+                    start=True,
+                    stop=True,
+                )
+                accs[(1, m, hn)] = acc
+
+        def Ev1(m, hn, engine):
+            if outs.get((1, m)) is None:
+                outs[(1, m)] = rot.tile([P, D_IN], F32, name="o1", tag="o1", bufs=5)
+            copy(engine, outs[(1, m)][:, HALF * hn : HALF * (hn + 1)], accs[(1, m, hn)][:])
+
+        def St1(m):
+            nc.sync.dma_start(out=out_1[P * m : P * (m + 1), :], in_=outs[(1, m)][:])
+
+        worder = [(0, 0), (1, 0), (0, 1), (1, 1)]
+
+        def MM0(hn, s):
+            x, g = worder[s]
+            cw, sw = codes["w%d%d%d" % (x, g, hn)]
+            for j in range(PACK):
+                if s == 0:
+                    accs[(0, j, hn)] = psum.tile([P, HALF], F32, name="bank", tag="bank")
+                fc, fs = codes["f%d%d" % (g, j // 2)]
+                c0 = (x * 2 + j % 2) * P
+                nc.tensor.matmul_mx(
+                    out=accs[(0, j, hn)][:],
+                    lhsT=fc[:, c0 : c0 + P].bitcast(E5),
+                    lhsT_scale=fs[:, c0 : c0 + P],
+                    rhs=cw[:].bitcast(E4),
+                    rhs_scale=sw[:],
+                    start=(s == 0),
+                    stop=(s == 3),
+                )
+
+        def Ev0(hn, j, engine):
+            outs[(0, hn, j)] = rot.tile([P, HALF], F32, name="o0", tag="o0", bufs=4)
+            copy(engine, outs[(0, hn, j)][:], accs[(0, j, hn)][:])
+
+        def St0(hn, j):
+            nc.sync.dma_start(out=o0_v[:, j, HALF * hn : HALF * (hn + 1)], in_=outs[(0, hn, j)][:])
+
+        ident = keep.tile([P, P], F32, name="ident")
+        make_identity(nc, ident[:])
+
+        L_ga(1, 2, 2)
+        EA(1, 2)
+        L_ch(1, 2, 2)
+        L_i("i1", 1, 0, 512)
+        L_ga(0, 2, 2)
+        L_ch(0, 2, 2)
+        L_ch(0, 0, 1)
+        EB(1, 2)
+        EC(1, 2)
+        T(1, 1)
+        EA(0, 2)
+        IL("i1", "S")
+        L_i("i0a", 0, 0, 256)
+        EB(0, 2)
+        L_i("i0b", 0, 256, 256)
+        EC(0, 2)
+        T(0, 1)
+        EvT(1, 1, 0, "S")
+        L_ga(0, 1, 1)
+        Q("i1")
+        EvT(1, 1, 1, "S")
+        L_ch(0, 1, 1)
+        EB(0, 1)
+        EA(0, 1)
+        L_ga(0, 0, 1)
+        EA(0, 0)
+        EvT(1, 1, 2, "S")
+        EB(0, 0)
+        L_w(1, 0)
+        EC(0, 1)
+        L_ga(1, 0, 2)
+        IL("i0a", "S")
+        L_ch(1, 0, 2)
+        L_w(0, 0)
+        EC(0, 0)
+        IL("i0b", "S")
+        EvT(0, 1, 1, "S")
+        Q("i0a")
+        Q("f11")
+        EvT(0, 1, 0, "S")
+        EA(1, 0)
+        L_w(0, 1)
+        EB(1, 0)
+        EvT(0, 1, 2, "S")
+        L_w(1, 1)
+        T(0, 0)
+        EC(1, 0)
+        Q("f01")
+        T(1, 0)
+        Q("i0b")
+        IL("w100", "S")
+        IL("t0", "S")
+        EvT(0, 0, 0, "S")
+        EvT(0, 0, 1, "S")
+        EvT(1, 0, 0, "S")
+        Q("t0")
+        MM1(2)
+        EvT(0, 0, 2, "S")
+        IL("w000", "V")
+        EvT(1, 0, 2, "S")
+        IL("t1", "V")
+        EvT(1, 0, 1, "S")
+        Q("w100")
+        Ev1(2, 0, "S")
+        MM1(1)
+        Q("t1")
+        IL("w001", "V")
+        MM1(4)
+        MM1(6)
+        Ev1(2, 1, "S")
+        St1(2)
+        Ev1(1, 1, "S")
+        IL("w010", "V")
+        MM1(0)
+        Ev1(1, 0, "S")
+        St1(1)
+        Ev1(4, 0, "S")
+        Q("w000")
+        Ev1(4, 1, "S")
+        St1(4)
+        Q("f00")
+        MM1(3)
+        Ev1(0, 0, "S")
+        Ev1(3, 1, "S")
+        Ev1(6, 1, "S")
+        Ev1(6, 0, "S")
+        St1(6)
+        Ev1(0, 1, "S")
+        St1(0)
+        MM1(7)
+        Ev1(3, 0, "V")
+        St1(3)
+        Q("f10")
+        MM1(5)
+        IL("w110", "V")
+        MM0(0, 0)
+        Ev1(7, 0, "S")
+        Ev1(7, 1, "S")
+        St1(7)
+        Q("w010")
+        Q("w110")
+        Ev1(5, 0, "S")
+        MM0(0, 1)
+        MM0(0, 2)
+        MM0(0, 3)
+        Ev1(5, 1, "S")
+        St1(5)
+        IL("w011", "S")
+        IL("w101", "V")
+        Q("w001")
+        Ev0(0, 0, "S")
+        St0(0, 0)
+        Q("w101")
+        Ev0(0, 2, "S")
+        St0(0, 2)
+        Q("w011")
+        IL("w111", "V")
+        MM0(1, 0)
+        Ev0(0, 1, "S")
+        St0(0, 1)
+        MM0(1, 1)
+        MM0(1, 2)
+        Ev0(0, 3, "S")
+        St0(0, 3)
+        Q("w111")
+        MM0(1, 3)
+        Ev0(1, 0, "V")
+        St0(1, 0)
+        Ev0(1, 1, "S")
+        St0(1, 1)
+        Ev0(1, 2, "S")
+        St0(1, 2)
+        Ev0(1, 3, "S")
+        St0(1, 3)

@@ -106,7 +106,7 @@ def tile_lstmcell_pa_v_kernel(
         def IL(u, engine):
             nn = dest[u][2]
             t = rot.tile([P, nn, PACK], BF16, name="il", tag="il", bufs=8, align_bytes=64)
-            copy(engine, t[:], src[u].rearrange("p j n -> p n j"))
+            copy(engine, t[:].rearrange("p (c i) j -> p c j i", i=4), src[u].rearrange("p j (c i) -> p c j i", i=4))
             il[u] = t[:].rearrange("p n j -> p (n j)")
 
         def Q(u):

@@ -52,7 +52,6 @@ def tile_lstmcell_pa_v_kernel(
         ch_u = {}
         v_u = {}
         dcf_u = {}
-        dcf_j = {}
         src = {}
         il = {}
         dest = {}
@@ -61,6 +60,8 @@ def tile_lstmcell_pa_v_kernel(
         fqs = {}
         accs = {}
         outs = {}
+        pils = {}
+        ilt = {}
 
         def new_codes(name):
             c = keep.tile([P, HALF], U32, name="c%s" % name, align_bytes=64)
@@ -92,6 +93,7 @@ def tile_lstmcell_pa_v_kernel(
                 dest[u] = (u, 0, HALF)
 
         dzi_h = [keep.tile([P, PACK, HALF], BF16, name="dzi%d" % hf, align_bytes=64) for hf in range(2)]
+        dcb_h = [keep.tile([P, PACK, HALF], BF16, name="dcb%d" % hf, align_bytes=64) for hf in range(2)]
         for hf in range(2):
             src["t%d" % hf] = dzi_h[hf][:]
             new_codes("t%d" % hf)
@@ -109,6 +111,30 @@ def tile_lstmcell_pa_v_kernel(
             copy(engine, t[:].rearrange("p (c i) j -> p c j i", i=4), src[u].rearrange("p j (c i) -> p c j i", i=4))
             il[u] = t[:].rearrange("p n j -> p (n j)")
 
+        def PIL(u):
+            nn = dest[u][2]
+            banks = []
+            for b in range(nn // 256):
+                pb = psum.tile([P, 256, PACK], BF16, name="bank", tag="bank")
+                for hh in range(2):
+                    n0 = 256 * b + P * hh
+                    nc.tensor.matmul(
+                        out=pb[:, P * hh : P * (hh + 1), :],
+                        lhsT=ident_b[:],
+                        rhs=src[u][:, :, n0 : n0 + P].rearrange("p j n -> p n j"),
+                        start=True,
+                        stop=True,
+                    )
+                banks.append(pb)
+            pils[u] = banks
+
+        def EvP(u, b, engine):
+            nn = dest[u][2]
+            if ilt.get(u) is None:
+                ilt[u] = rot.tile([P, nn, PACK], BF16, name="il", tag="il", bufs=8, align_bytes=64)
+                il[u] = ilt[u][:].rearrange("p n j -> p (n j)")
+            copy(engine, ilt[u][:, 256 * b : 256 * (b + 1), :], pils[u][b][:])
+
         def Q(u):
             name, n0, nn = dest[u]
             fmt = E4 if u[0] in "iw" else E5
@@ -121,8 +147,11 @@ def tile_lstmcell_pa_v_kernel(
             dcf = keep.tile([P, nj, HALF], F32, name="dcf%d%d" % k)
             nc.vector.tensor_tensor(out=dcf[:], in0=g_u[k][:], in1=ig_u[k][:], op=MULT)
             dcf_u[k] = dcf
-            for jj in range(nj):
-                dcf_j[(hf, j0 + jj)] = dcf[:, jj, :]
+
+        def CA(hf, j0, engine):
+            k = (hf, j0)
+            nj = g_u[k].shape[1]
+            copy(engine, dcb_h[hf][:, j0 : j0 + nj, :], dcf_u[k][:])
 
         def EB(hf, j0):
             k = (hf, j0)
@@ -140,17 +169,14 @@ def tile_lstmcell_pa_v_kernel(
 
         def T(hf, jp):
             k = (hf, jp)
-            tz = psum.tile([P, 2, 2, P], F32, name="bank", tag="bank")
-            for jj in range(2):
-                words = dzi_h[hf][:, 2 * jp + jj, :].bitcast(F32)
-                for u in range(2):
-                    nc.tensor.transpose(tz[:, jj, u, :], words[:, u : HALF // 2 : 2], ident[:])
-            banks = [tz]
-            for jj in range(2):
-                tcx = psum.tile([P, PACK, P], F32, name="bank", tag="bank")
-                for t in range(PACK):
-                    nc.tensor.transpose(tcx[:, t, :], dcf_j[(hf, 2 * jp + jj)][:, t:HALF:PACK], ident[:])
-                banks.append(tcx)
+            banks = []
+            for x in range(2):
+                bank = psum.tile([P, 2, 2, P], F32, name="bank", tag="bank")
+                for jj in range(2):
+                    words = (dzi_h, dcb_h)[x][hf][:, 2 * jp + jj, :].bitcast(F32)
+                    for u in range(2):
+                        nc.tensor.transpose(bank[:, jj, u, :], words[:, u : HALF // 2 : 2], ident[:])
+                banks.append(bank)
             tps[k] = banks
             f = keep.tile([P, 2, 2, P, PACK], BF16, name="fq%d%d" % k, align_bytes=64)
             fqs[k] = f
@@ -162,10 +188,7 @@ def tile_lstmcell_pa_v_kernel(
         def EvT(hf, jp, i, engine):
             k = (hf, jp)
             f = fqs[k]
-            if i == 0:
-                copy(engine, f[:, 0, :, :, :].bitcast(F32), tps[k][0][:].rearrange("p j u r -> p j r u"))
-            else:
-                copy(engine, f[:, 1, i - 1, :, :], tps[k][i][:].rearrange("p t r -> p r t"))
+            copy(engine, f[:, i, :, :, :].bitcast(F32), tps[k][i][:].rearrange("p j u r -> p j r u"))
 
         def MM1(m):
             hf, mm = divmod(m, 4)
@@ -222,134 +245,141 @@ def tile_lstmcell_pa_v_kernel(
 
         ident = keep.tile([P, P], F32, name="ident")
         make_identity(nc, ident[:])
+        ident_b = keep.tile([P, P], BF16, name="identb")
+        make_identity(nc, ident_b[:])
 
         L_ga(1, 2, 2)
         EA(1, 2)
         L_ch(1, 2, 2)
-        L_i("i1", 1, 0, 512)
-        L_ga(0, 2, 2)
-        L_ch(0, 2, 2)
-        L_ch(0, 0, 1)
-        EB(1, 2)
-        EC(1, 2)
-        T(1, 1)
-        EA(0, 2)
-        IL("i1", "S")
-        L_i("i0a", 0, 0, 256)
-        EB(0, 2)
-        L_i("i0b", 0, 256, 256)
-        EC(0, 2)
-        T(0, 1)
-        EvT(1, 1, 0, "S")
-        L_ga(0, 1, 1)
-        Q("i1")
-        EvT(1, 1, 1, "S")
-        L_ch(0, 1, 1)
-        EB(0, 1)
-        EA(0, 1)
-        L_ga(0, 0, 1)
-        EA(0, 0)
-        EvT(1, 1, 2, "S")
-        EB(0, 0)
-        L_w(1, 0)
-        EC(0, 1)
         L_ga(1, 0, 2)
-        IL("i0a", "S")
+        L_i("i0a", 0, 0, 256)
+        EB(1, 2)
         L_ch(1, 0, 2)
-        L_w(0, 0)
-        EC(0, 0)
-        IL("i0b", "S")
-        EvT(0, 1, 1, "S")
-        Q("i0a")
-        Q("f11")
-        EvT(0, 1, 0, "S")
+        EC(1, 2)
+        CA(1, 2, "S")
+        L_ga(0, 2, 2)
         EA(1, 0)
-        L_w(0, 1)
+        IL("i0a", "S")
+        L_i("i0b", 0, 256, 256)
+        CA(1, 0, "S")
+        T(1, 1)
+        EvT(1, 1, 1, "S")
+        EvT(1, 1, 0, "S")
         EB(1, 0)
-        EvT(0, 1, 2, "S")
-        L_w(1, 1)
-        T(0, 0)
+        L_ch(0, 2, 2)
+        IL("i0b", "S")
         EC(1, 0)
-        Q("f01")
+        PIL("t1")
+        L_i("i1", 1, 0, 512)
+        L_ga(0, 1, 1)
+        EA(0, 2)
+        CA(0, 2, "S")
+        IL("i1", "S")
+        EvP("t1", 0, "S")
+        L_ga(0, 0, 1)
         T(1, 0)
-        Q("i0b")
-        IL("w100", "S")
-        IL("t0", "S")
-        EvT(0, 0, 0, "S")
-        EvT(0, 0, 1, "S")
+        EB(0, 2)
+        EC(0, 2)
+        EA(0, 1)
+        L_ch(0, 0, 1)
+        EA(0, 0)
+        T(0, 1)
+        L_w(1, 0)
+        Q("i0a")
+        EB(0, 0)
+        CA(0, 1, "S")
+        L_ch(0, 1, 1)
+        EvP("t1", 1, "S")
+        PIL("w100")
+        EC(0, 0)
+        Q("f11")
+        CA(0, 0, "S")
+        Q("i1")
+        EvT(0, 1, 1, "S")
+        EB(0, 1)
+        EC(0, 1)
+        L_w(0, 0)
+        IL("t0", "V")
         EvT(1, 0, 0, "S")
+        EvT(1, 0, 1, "S")
+        Q("i0b")
+        EvT(0, 1, 0, "S")
+        T(0, 0)
+        L_w(0, 1)
         Q("t0")
         MM1(2)
-        EvT(0, 0, 2, "S")
-        IL("w000", "V")
-        EvT(1, 0, 2, "S")
-        IL("t1", "V")
-        EvT(1, 0, 1, "S")
-        Q("w100")
-        Ev1(2, 0, "S")
-        MM1(1)
+        EvP("w100", 1, "V")
         Q("t1")
-        IL("w001", "V")
-        MM1(4)
         MM1(6)
+        Q("f01")
+        EvP("w100", 0, "S")
+        IL("w000", "S")
+        EvT(0, 0, 1, "S")
+        MM1(1)
+        EvT(0, 0, 0, "V")
+        Ev1(2, 0, "V")
+        MM1(0)
+        IL("w010", "V")
+        L_w(1, 1)
         Ev1(2, 1, "S")
         St1(2)
-        Ev1(1, 1, "S")
-        IL("w010", "V")
-        MM1(0)
-        Ev1(1, 0, "S")
-        St1(1)
-        Ev1(4, 0, "S")
-        Q("w000")
-        Ev1(4, 1, "S")
-        St1(4)
-        Q("f00")
-        MM1(3)
-        Ev1(0, 0, "S")
-        Ev1(3, 1, "S")
-        Ev1(6, 1, "S")
+        Ev1(0, 1, "V")
         Ev1(6, 0, "S")
+        Q("f00")
+        Ev1(1, 0, "S")
+        Ev1(6, 1, "S")
         St1(6)
-        Ev1(0, 1, "S")
+        Ev1(0, 0, "S")
         St1(0)
-        MM1(7)
-        Ev1(3, 0, "V")
-        St1(3)
-        Q("f10")
+        Q("w100")
+        MM1(3)
+        Ev1(1, 1, "S")
+        St1(1)
         MM1(5)
-        IL("w110", "V")
-        MM0(0, 0)
-        Ev1(7, 0, "S")
-        Ev1(7, 1, "S")
-        St1(7)
-        Q("w010")
-        Q("w110")
+        Ev1(3, 0, "S")
+        Ev1(3, 1, "S")
+        St1(3)
         Ev1(5, 0, "S")
+        Ev1(5, 1, "V")
+        St1(5)
+        MM1(7)
+        Q("w000")
+        IL("w110", "V")
+        IL("w011", "S")
+        MM1(4)
+        Q("w010")
+        MM0(0, 0)
+        Q("f10")
         MM0(0, 1)
         MM0(0, 2)
+        IL("w001", "V")
+        Ev1(4, 1, "S")
+        Q("w110")
+        Ev1(7, 0, "S")
+        Ev1(4, 0, "S")
+        St1(4)
         MM0(0, 3)
-        Ev1(5, 1, "S")
-        St1(5)
-        IL("w011", "S")
-        IL("w101", "V")
         Q("w001")
+        Ev1(7, 1, "S")
+        St1(7)
         Ev0(0, 0, "S")
         St0(0, 0)
-        Q("w101")
-        Ev0(0, 2, "S")
-        St0(0, 2)
-        Q("w011")
-        IL("w111", "V")
-        MM0(1, 0)
         Ev0(0, 1, "S")
         St0(0, 1)
+        IL("w111", "S")
+        IL("w101", "V")
+        Q("w101")
+        Q("w011")
+        Ev0(0, 3, "V")
+        St0(0, 3)
+        Ev0(0, 2, "V")
+        St0(0, 2)
+        MM0(1, 0)
         MM0(1, 1)
         MM0(1, 2)
-        Ev0(0, 3, "S")
-        St0(0, 3)
         Q("w111")
         MM0(1, 3)
-        Ev0(1, 0, "V")
+        Ev0(1, 0, "S")
         St0(1, 0)
         Ev0(1, 1, "S")
         St0(1, 1)

@@ -3,387 +3,378 @@ from contextlib import ExitStack
 import concourse.mybir as mybir
 from concourse.masks import make_identity
 
-B, D_IN, D_H = 512, 1024, 1024
-FLOPS = 2 * B * D_H * D_IN * 3
-BYTES = 2 * B * D_IN + 2 * 2 * D_H * D_IN + 2 * 4 * B * D_H + 2 * B * D_H + 4 * B * D_IN + 4 * D_H * D_IN
+TOKENS, D_IN, D_H = 512, 1024, 1024
+FLOPS = 2 * TOKENS * D_H * D_IN * 3
+BYTES = (
+    2 * TOKENS * D_IN + 2 * 2 * D_H * D_IN + 2 * 4 * TOKENS * D_H + 2 * TOKENS * D_H + 4 * TOKENS * D_IN + 4 * D_H * D_IN
+)
 
 F32 = mybir.dt.float32
 BF16 = mybir.dt.bfloat16
 U32 = mybir.dt.uint32
 U8 = mybir.dt.uint8
-E4 = mybir.dt.float8_e4m3fn_x4
-E5 = mybir.dt.float8_e5m2_x4
+E4M3 = mybir.dt.float8_e4m3fn_x4
+E5M2 = mybir.dt.float8_e5m2_x4
 MULT = mybir.AluOpType.mult
-SUB = mybir.AluOpType.subtract
+SUBTRACT = mybir.AluOpType.subtract
 
 P = 128
 PACK = 4
 HALF = 512
+BANKS = 8
+STAGING = 8
+OUT1_TILES = 5
+OUT0_TILES = 4
 
 
 def tile_lstmcell_pa_v_kernel(
     tc, incoming, h, W_i, b_W_i, W_c, b_W_c, U_i, b_U_i, U_c, b_U_c, I_gate, C_head, grad_out, out_0, out_1
 ):
     nc = tc.nc
+    on_vector = nc.vector.tensor_copy
+    on_scalar = nc.scalar.copy
+
     with ExitStack() as ctx:
         raw = ctx.enter_context(tc.tile_pool(name="raw", bufs=1))
         keep = ctx.enter_context(tc.tile_pool(name="keep", bufs=1))
         rot = ctx.enter_context(tc.tile_pool(name="rot", bufs=2))
-        psum = ctx.enter_context(tc.psum_pool(name="psum", bufs=8))
+        psum = ctx.enter_context(tc.psum_pool(name="psum", bufs=BANKS))
         ctx.enter_context(tc.manual_schedule())
 
-        g_v = grad_out.rearrange("(p j) w -> p j w", j=PACK)
-        ig_v = I_gate.rearrange("(p j) w -> p j w", j=PACK)
-        ch_v = C_head.rearrange("(p j) w -> p j w", j=PACK)
-        inc_v = incoming.rearrange("(p j) n -> p j n", j=PACK)
-        w_v = [
+        grad_view = grad_out.rearrange("(p j) w -> p j w", j=PACK)
+        gate_view = I_gate.rearrange("(p j) w -> p j w", j=PACK)
+        cand_view = C_head.rearrange("(p j) w -> p j w", j=PACK)
+        incoming_view = incoming.rearrange("(p j) n -> p j n", j=PACK)
+        weight_view = [
             W_i.rearrange("(g p j) n -> p g j n", g=2, j=PACK),
             W_c.rearrange("(g p j) n -> p g j n", g=2, j=PACK),
         ]
-        o0_v = out_0.rearrange("(p j) n -> p j n", j=PACK)
+        out0_view = out_0.rearrange("(p j) n -> p j n", j=PACK)
+
+        grad = {}
+        gate = {}
+        cand = {}
+        slope = {}
+        dc32 = {}
+        dc32_slot = {}
+        rows = {}
+        grouped = {}
+        place = {}
+        codes = {}
+        banks = {}
+        transposed = {}
+        staged = {}
+        result = {}
 
         def load(view, shape, dtype, name):
-            t = raw.tile(shape, dtype, name=name)
-            nc.sync.dma_start(out=t[:], in_=view)
-            return t
-
-        g_u = {}
-        ig_u = {}
-        ch_u = {}
-        v_u = {}
-        dcf_u = {}
-        src = {}
-        il = {}
-        dest = {}
-        codes = {}
-        tps = {}
-        fqs = {}
-        accs = {}
-        outs = {}
-        pils = {}
-        ilt = {}
+            tile = raw.tile(shape, dtype, name=name)
+            nc.sync.dma_start(out=tile[:], in_=view)
+            return tile
 
         def new_codes(name):
-            c = keep.tile([P, HALF], U32, name="c%s" % name, align_bytes=64)
-            s = keep.tile([P, HALF], U8, name="s%s" % name, align_bytes=64)
-            codes[name] = (c, s)
+            words = keep.tile([P, HALF], U32, name="c%s" % name, align_bytes=64)
+            scales = keep.tile([P, HALF], U8, name="s%s" % name, align_bytes=64)
+            codes[name] = (words, scales)
 
-        def L_ga(hf, j0, nj):
-            ws = slice(HALF * hf, HALF * (hf + 1))
-            g_u[(hf, j0)] = load(g_v[:, j0 : j0 + nj, ws], [P, nj, HALF], BF16, "g%d%d" % (hf, j0))
-            ig_u[(hf, j0)] = load(ig_v[:, j0 : j0 + nj, ws], [P, nj, HALF], F32, "ig%d%d" % (hf, j0))
+        def load_grad_gate(half, j0, slots):
+            features = slice(HALF * half, HALF * (half + 1))
+            unit = (half, j0)
+            grad[unit] = load(grad_view[:, j0 : j0 + slots, features], [P, slots, HALF], BF16, "g%d%d" % unit)
+            gate[unit] = load(gate_view[:, j0 : j0 + slots, features], [P, slots, HALF], F32, "ig%d%d" % unit)
 
-        def L_ch(hf, j0, nj):
-            ws = slice(HALF * hf, HALF * (hf + 1))
-            ch_u[(hf, j0)] = load(ch_v[:, j0 : j0 + nj, ws], [P, nj, HALF], F32, "ch%d%d" % (hf, j0))
+        def load_cand(half, j0, slots):
+            features = slice(HALF * half, HALF * (half + 1))
+            cand[(half, j0)] = load(cand_view[:, j0 : j0 + slots, features], [P, slots, HALF], F32, "ch%d%d" % (half, j0))
 
-        def L_i(u, hn, n0, nn):
-            t = load(inc_v[:, :, HALF * hn + n0 : HALF * hn + n0 + nn], [P, PACK, nn], BF16, u)
-            src[u] = t[:]
-            if codes.get("i%d" % hn) is None:
-                new_codes("i%d" % hn)
-            dest[u] = ("i%d" % hn, n0, nn)
+        def load_incoming(name, n_half, first, columns):
+            start = HALF * n_half + first
+            rows[name] = load(incoming_view[:, :, start : start + columns], [P, PACK, columns], BF16, name)[:]
+            if codes.get("i%d" % n_half) is None:
+                new_codes("i%d" % n_half)
+            place[name] = ("i%d" % n_half, first, columns)
 
-        def L_w(x, g):
-            t = load(w_v[x][:, g, :, :], [P, PACK, D_IN], BF16, "w%d%d" % (x, g))
-            for hn in range(2):
-                u = "w%d%d%d" % (x, g, hn)
-                src[u] = t[:, :, HALF * hn : HALF * (hn + 1)]
-                new_codes(u)
-                dest[u] = (u, 0, HALF)
+        def load_weight(which, g):
+            tile = load(weight_view[which][:, g, :, :], [P, PACK, D_IN], BF16, "w%d%d" % (which, g))
+            for n_half in range(2):
+                name = "w%d%d%d" % (which, g, n_half)
+                rows[name] = tile[:, :, HALF * n_half : HALF * (n_half + 1)]
+                new_codes(name)
+                place[name] = (name, 0, HALF)
 
-        dzi_h = [keep.tile([P, PACK, HALF], BF16, name="dzi%d" % hf, align_bytes=64) for hf in range(2)]
-        dcb_h = [keep.tile([P, PACK, HALF], BF16, name="dcb%d" % hf, align_bytes=64) for hf in range(2)]
-        for hf in range(2):
-            src["t%d" % hf] = dzi_h[hf][:]
-            new_codes("t%d" % hf)
-            dest["t%d" % hf] = ("t%d" % hf, 0, HALF)
+        dzi = [keep.tile([P, PACK, HALF], BF16, name="dzi%d" % half, align_bytes=64) for half in range(2)]
+        for half in range(2):
+            rows["t%d" % half] = dzi[half][:]
+            new_codes("t%d" % half)
+            place["t%d" % half] = ("t%d" % half, 0, HALF)
 
-        def copy(engine, out, in_):
-            if engine == "V":
-                nc.vector.tensor_copy(out=out, in_=in_)
-            else:
-                nc.scalar.copy(out=out, in_=in_)
+        def interleave(name, copy):
+            tile = rot.tile([P, place[name][2], PACK], BF16, name="il", tag="il", bufs=STAGING, align_bytes=64)
+            copy(
+                out=tile[:].rearrange("p (c i) j -> p c j i", i=4),
+                in_=rows[name].rearrange("p j (c i) -> p c j i", i=4),
+            )
+            grouped[name] = tile[:].rearrange("p n j -> p (n j)")
 
-        def IL(u, engine):
-            nn = dest[u][2]
-            t = rot.tile([P, nn, PACK], BF16, name="il", tag="il", bufs=8, align_bytes=64)
-            copy(engine, t[:].rearrange("p (c i) j -> p c j i", i=4), src[u].rearrange("p j (c i) -> p c j i", i=4))
-            il[u] = t[:].rearrange("p n j -> p (n j)")
-
-        def PIL(u):
-            nn = dest[u][2]
-            banks = []
-            for b in range(nn // 256):
-                pb = psum.tile([P, 256, PACK], BF16, name="bank", tag="bank")
-                for hh in range(2):
-                    n0 = 256 * b + P * hh
+        def interleave_on_tensor(name):
+            banks[name] = []
+            for b in range(place[name][2] // (2 * P)):
+                bank = psum.tile([P, 2 * P, PACK], BF16, name="bank", tag="bank")
+                for part in range(2):
+                    first = 2 * P * b + P * part
                     nc.tensor.matmul(
-                        out=pb[:, P * hh : P * (hh + 1), :],
-                        lhsT=ident_b[:],
-                        rhs=src[u][:, :, n0 : n0 + P].rearrange("p j n -> p n j"),
+                        out=bank[:, P * part : P * (part + 1), :],
+                        lhsT=identity_bf16[:],
+                        rhs=rows[name][:, :, first : first + P].rearrange("p j n -> p n j"),
                         start=True,
                         stop=True,
                     )
-                banks.append(pb)
-            pils[u] = banks
+                banks[name].append(bank)
 
-        def EvP(u, b, engine):
-            nn = dest[u][2]
-            if ilt.get(u) is None:
-                ilt[u] = rot.tile([P, nn, PACK], BF16, name="il", tag="il", bufs=8, align_bytes=64)
-                il[u] = ilt[u][:].rearrange("p n j -> p (n j)")
-            copy(engine, ilt[u][:, 256 * b : 256 * (b + 1), :], pils[u][b][:])
+        def copy_interleaved(name, b, copy):
+            if staged.get(name) is None:
+                staged[name] = rot.tile([P, place[name][2], PACK], BF16, name="il", tag="il", bufs=STAGING, align_bytes=64)
+                grouped[name] = staged[name][:].rearrange("p n j -> p (n j)")
+            copy(out=staged[name][:, 2 * P * b : 2 * P * (b + 1), :], in_=banks[name][b][:])
 
-        def Q(u):
-            name, n0, nn = dest[u]
-            fmt = E4 if u[0] in "iw" else E5
-            c, s = codes[name]
-            nc.vector.quantize_mx(out=c[:, n0 : n0 + nn].bitcast(fmt), scales=s[:, n0 : n0 + nn], in_=il[u])
-
-        def EA(hf, j0):
-            k = (hf, j0)
-            nj = g_u[k].shape[1]
-            dcf = keep.tile([P, nj, HALF], F32, name="dcf%d%d" % k)
-            nc.vector.tensor_tensor(out=dcf[:], in0=g_u[k][:], in1=ig_u[k][:], op=MULT)
-            dcf_u[k] = dcf
-
-        def CA(hf, j0, engine):
-            k = (hf, j0)
-            nj = g_u[k].shape[1]
-            copy(engine, dcb_h[hf][:, j0 : j0 + nj, :], dcf_u[k][:])
-
-        def EB(hf, j0):
-            k = (hf, j0)
-            nj = g_u[k].shape[1]
-            v = rot.tile([P, nj, HALF], F32, name="v", tag="v", bufs=2)
-            nc.vector.scalar_tensor_tensor(out=v[:], in0=ig_u[k][:], scalar=1.0, in1=ch_u[k][:], op0=SUB, op1=MULT)
-            v_u[k] = v
-
-        def EC(hf, j0):
-            k = (hf, j0)
-            nj = g_u[k].shape[1]
-            nc.vector.scalar_tensor_tensor(
-                out=dzi_h[hf][:, j0 : j0 + nj, :], in0=v_u[k][:], scalar=-1.0, in1=dcf_u[k][:], op0=MULT, op1=MULT
+        def quantize(name):
+            operand, first, columns = place[name]
+            fmt = E4M3 if name[0] in "iw" else E5M2
+            words, scales = codes[operand]
+            nc.vector.quantize_mx(
+                out=words[:, first : first + columns].bitcast(fmt),
+                scales=scales[:, first : first + columns],
+                in_=grouped[name],
             )
 
-        def T(hf, jp):
-            k = (hf, jp)
-            banks = []
-            for x in range(2):
-                bank = psum.tile([P, 2, 2, P], F32, name="bank", tag="bank")
-                for jj in range(2):
-                    words = (dzi_h, dcb_h)[x][hf][:, 2 * jp + jj, :].bitcast(F32)
-                    for u in range(2):
-                        nc.tensor.transpose(bank[:, jj, u, :], words[:, u : HALF // 2 : 2], ident[:])
-                banks.append(bank)
-            tps[k] = banks
-            f = keep.tile([P, 2, 2, P, PACK], BF16, name="fq%d%d" % k, align_bytes=64)
-            fqs[k] = f
-            u = "f%d%d" % k
-            il[u] = f[:].rearrange("p x j r t -> p (x j r t)")
-            new_codes(u)
-            dest[u] = (u, 0, HALF)
+        def dc_product(half, j0):
+            unit = (half, j0)
+            dc32[unit] = keep.tile([P, grad[unit].shape[1], HALF], F32, name="dcf%d%d" % unit)
+            nc.vector.tensor_tensor(out=dc32[unit][:], in0=grad[unit][:], in1=gate[unit][:], op=MULT)
+            for jj in range(grad[unit].shape[1]):
+                dc32_slot[(half, j0 + jj)] = dc32[unit][:, jj, :]
 
-        def EvT(hf, jp, i, engine):
-            k = (hf, jp)
-            f = fqs[k]
-            copy(engine, f[:, i, :, :, :].bitcast(F32), tps[k][i][:].rearrange("p j u r -> p j r u"))
+        def gate_slope(half, j0):
+            unit = (half, j0)
+            slope[unit] = rot.tile([P, grad[unit].shape[1], HALF], F32, name="v", tag="v", bufs=2)
+            nc.vector.scalar_tensor_tensor(
+                out=slope[unit][:], in0=gate[unit][:], scalar=1.0, in1=cand[unit][:], op0=SUBTRACT, op1=MULT
+            )
 
-        def MM1(m):
-            hf, mm = divmod(m, 4)
-            cols = slice(P * mm, P * (mm + 1))
-            c, s = codes["t%d" % hf]
-            for hn in range(2):
-                acc = psum.tile([P, HALF], F32, name="bank", tag="bank")
-                ci, si = codes["i%d" % hn]
+        def dzi_product(half, j0):
+            unit = (half, j0)
+            nc.vector.scalar_tensor_tensor(
+                out=dzi[half][:, j0 : j0 + grad[unit].shape[1], :],
+                in0=slope[unit][:],
+                scalar=-1.0,
+                in1=dc32[unit][:],
+                op0=MULT,
+                op1=MULT,
+            )
+
+        def transpose_pair(half, pair):
+            unit = (half, pair)
+            dzi_bank = psum.tile([P, 2, 2, P], F32, name="bank", tag="bank")
+            for jj in range(2):
+                words = dzi[half][:, 2 * pair + jj, :].bitcast(F32)
+                for u in range(2):
+                    nc.tensor.transpose(dzi_bank[:, jj, u, :], words[:, u : HALF // 2 : 2], identity[:])
+            banks[unit] = [dzi_bank]
+            for jj in range(2):
+                dc_bank = psum.tile([P, PACK, P], F32, name="bank", tag="bank")
+                for t in range(PACK):
+                    nc.tensor.transpose(dc_bank[:, t, :], dc32_slot[(half, 2 * pair + jj)][:, t:HALF:PACK], identity[:])
+                banks[unit].append(dc_bank)
+            transposed[unit] = keep.tile([P, 2, 2, P, PACK], BF16, name="fq%d%d" % unit, align_bytes=64)
+            name = "f%d%d" % unit
+            grouped[name] = transposed[unit][:].rearrange("p x j r t -> p (x j r t)")
+            new_codes(name)
+            place[name] = (name, 0, HALF)
+
+        def copy_transposed(half, pair, bank, copy):
+            unit = (half, pair)
+            if bank == 0:
+                copy(
+                    out=transposed[unit][:, 0, :, :, :].bitcast(F32),
+                    in_=banks[unit][0][:].rearrange("p j u r -> p j r u"),
+                )
+            else:
+                copy(out=transposed[unit][:, 1, bank - 1, :, :], in_=banks[unit][bank][:].rearrange("p t r -> p r t"))
+
+        def out1_matmuls(m):
+            half, mm = divmod(m, 4)
+            features = slice(P * mm, P * (mm + 1))
+            dzi_words, dzi_scales = codes["t%d" % half]
+            for n_half in range(2):
+                bank = psum.tile([P, HALF], F32, name="bank", tag="bank")
+                inc_words, inc_scales = codes["i%d" % n_half]
                 nc.tensor.matmul_mx(
-                    out=acc[:],
-                    lhsT=c[:, cols].bitcast(E5),
-                    lhsT_scale=s[:, cols],
-                    rhs=ci[:].bitcast(E4),
-                    rhs_scale=si[:],
+                    out=bank[:],
+                    lhsT=dzi_words[:, features].bitcast(E5M2),
+                    lhsT_scale=dzi_scales[:, features],
+                    rhs=inc_words[:].bitcast(E4M3),
+                    rhs_scale=inc_scales[:],
                     start=True,
                     stop=True,
                 )
-                accs[(1, m, hn)] = acc
+                banks[(1, m, n_half)] = bank
 
-        def Ev1(m, hn, engine):
-            if outs.get((1, m)) is None:
-                outs[(1, m)] = rot.tile([P, D_IN], F32, name="o1", tag="o1", bufs=5)
-            copy(engine, outs[(1, m)][:, HALF * hn : HALF * (hn + 1)], accs[(1, m, hn)][:])
+        def out1_copy(m, n_half, copy):
+            if result.get(m) is None:
+                result[m] = [rot.tile([P, D_IN], F32, name="o1", tag="o1", bufs=OUT1_TILES)]
+            tile = result[m][0]
+            copy(out=tile[:, HALF * n_half : HALF * (n_half + 1)], in_=banks[(1, m, n_half)][:])
+            result[m].append(n_half)
+            if len(result[m]) == 3:
+                nc.sync.dma_start(out=out_1[P * m : P * (m + 1), :], in_=tile[:])
 
-        def St1(m):
-            nc.sync.dma_start(out=out_1[P * m : P * (m + 1), :], in_=outs[(1, m)][:])
+        passes = [(0, 0), (1, 0), (0, 1), (1, 1)]
 
-        worder = [(0, 0), (1, 0), (0, 1), (1, 1)]
-
-        def MM0(hn, s):
-            x, g = worder[s]
-            cw, sw = codes["w%d%d%d" % (x, g, hn)]
+        def out0_pass(n_half, s):
+            which, g = passes[s]
+            w_words, w_scales = codes["w%d%d%d" % (which, g, n_half)]
             for j in range(PACK):
                 if s == 0:
-                    accs[(0, j, hn)] = psum.tile([P, HALF], F32, name="bank", tag="bank")
-                fc, fs = codes["f%d%d" % (g, j // 2)]
-                c0 = (x * 2 + j % 2) * P
+                    banks[(0, j, n_half)] = psum.tile([P, HALF], F32, name="bank", tag="bank")
+                dz_words, dz_scales = codes["f%d%d" % (g, j // 2)]
+                first = (which * 2 + j % 2) * P
                 nc.tensor.matmul_mx(
-                    out=accs[(0, j, hn)][:],
-                    lhsT=fc[:, c0 : c0 + P].bitcast(E5),
-                    lhsT_scale=fs[:, c0 : c0 + P],
-                    rhs=cw[:].bitcast(E4),
-                    rhs_scale=sw[:],
+                    out=banks[(0, j, n_half)][:],
+                    lhsT=dz_words[:, first : first + P].bitcast(E5M2),
+                    lhsT_scale=dz_scales[:, first : first + P],
+                    rhs=w_words[:].bitcast(E4M3),
+                    rhs_scale=w_scales[:],
                     start=(s == 0),
-                    stop=(s == 3),
+                    stop=(s == len(passes) - 1),
                 )
 
-        def Ev0(hn, j, engine):
-            outs[(0, hn, j)] = rot.tile([P, HALF], F32, name="o0", tag="o0", bufs=4)
-            copy(engine, outs[(0, hn, j)][:], accs[(0, j, hn)][:])
+        def out0_copy(n_half, j, copy):
+            tile = rot.tile([P, HALF], F32, name="o0", tag="o0", bufs=OUT0_TILES)
+            copy(out=tile[:], in_=banks[(0, j, n_half)][:])
+            nc.sync.dma_start(out=out0_view[:, j, HALF * n_half : HALF * (n_half + 1)], in_=tile[:])
 
-        def St0(hn, j):
-            nc.sync.dma_start(out=o0_v[:, j, HALF * hn : HALF * (hn + 1)], in_=outs[(0, hn, j)][:])
+        identity = keep.tile([P, P], F32, name="ident")
+        make_identity(nc, identity[:])
+        identity_bf16 = keep.tile([P, P], BF16, name="identb")
+        make_identity(nc, identity_bf16[:])
 
-        ident = keep.tile([P, P], F32, name="ident")
-        make_identity(nc, ident[:])
-        ident_b = keep.tile([P, P], BF16, name="identb")
-        make_identity(nc, ident_b[:])
-
-        L_ga(1, 2, 2)
-        EA(1, 2)
-        L_ch(1, 2, 2)
-        L_ga(1, 0, 2)
-        L_i("i0a", 0, 0, 256)
-        EB(1, 2)
-        L_ch(1, 0, 2)
-        EC(1, 2)
-        CA(1, 2, "S")
-        L_ga(0, 2, 2)
-        EA(1, 0)
-        IL("i0a", "S")
-        L_i("i0b", 0, 256, 256)
-        CA(1, 0, "S")
-        T(1, 1)
-        EvT(1, 1, 1, "S")
-        EvT(1, 1, 0, "S")
-        EB(1, 0)
-        L_ch(0, 2, 2)
-        IL("i0b", "S")
-        EC(1, 0)
-        PIL("t1")
-        L_i("i1", 1, 0, 512)
-        L_ga(0, 1, 1)
-        EA(0, 2)
-        CA(0, 2, "S")
-        IL("i1", "S")
-        EvP("t1", 0, "S")
-        L_ga(0, 0, 1)
-        T(1, 0)
-        EB(0, 2)
-        EC(0, 2)
-        EA(0, 1)
-        L_ch(0, 0, 1)
-        EA(0, 0)
-        T(0, 1)
-        L_w(1, 0)
-        Q("i0a")
-        EB(0, 0)
-        CA(0, 1, "S")
-        L_ch(0, 1, 1)
-        EvP("t1", 1, "S")
-        PIL("w100")
-        EC(0, 0)
-        Q("f11")
-        CA(0, 0, "S")
-        Q("i1")
-        EvT(0, 1, 1, "S")
-        EB(0, 1)
-        EC(0, 1)
-        L_w(0, 0)
-        IL("t0", "V")
-        EvT(1, 0, 0, "S")
-        EvT(1, 0, 1, "S")
-        Q("i0b")
-        EvT(0, 1, 0, "S")
-        T(0, 0)
-        L_w(0, 1)
-        Q("t0")
-        MM1(2)
-        EvP("w100", 1, "V")
-        Q("t1")
-        MM1(6)
-        Q("f01")
-        EvP("w100", 0, "S")
-        IL("w000", "S")
-        EvT(0, 0, 1, "S")
-        MM1(1)
-        EvT(0, 0, 0, "V")
-        Ev1(2, 0, "V")
-        MM1(0)
-        IL("w010", "V")
-        L_w(1, 1)
-        Ev1(2, 1, "S")
-        St1(2)
-        Ev1(0, 1, "V")
-        Ev1(6, 0, "S")
-        Q("f00")
-        Ev1(1, 0, "S")
-        Ev1(6, 1, "S")
-        St1(6)
-        Ev1(0, 0, "S")
-        St1(0)
-        Q("w100")
-        MM1(3)
-        Ev1(1, 1, "S")
-        St1(1)
-        MM1(5)
-        Ev1(3, 0, "S")
-        Ev1(3, 1, "S")
-        St1(3)
-        Ev1(5, 0, "S")
-        Ev1(5, 1, "V")
-        St1(5)
-        MM1(7)
-        Q("w000")
-        IL("w110", "V")
-        IL("w011", "S")
-        MM1(4)
-        Q("w010")
-        MM0(0, 0)
-        Q("f10")
-        MM0(0, 1)
-        MM0(0, 2)
-        IL("w001", "V")
-        Ev1(4, 1, "S")
-        Q("w110")
-        Ev1(7, 0, "S")
-        Ev1(4, 0, "S")
-        St1(4)
-        MM0(0, 3)
-        Q("w001")
-        Ev1(7, 1, "S")
-        St1(7)
-        Ev0(0, 0, "S")
-        St0(0, 0)
-        Ev0(0, 1, "S")
-        St0(0, 1)
-        IL("w111", "S")
-        IL("w101", "V")
-        Q("w101")
-        Q("w011")
-        Ev0(0, 3, "V")
-        St0(0, 3)
-        Ev0(0, 2, "V")
-        St0(0, 2)
-        MM0(1, 0)
-        MM0(1, 1)
-        MM0(1, 2)
-        Q("w111")
-        MM0(1, 3)
-        Ev0(1, 0, "S")
-        St0(1, 0)
-        Ev0(1, 1, "S")
-        St0(1, 1)
-        Ev0(1, 2, "S")
-        St0(1, 2)
-        Ev0(1, 3, "S")
-        St0(1, 3)
+        load_grad_gate(1, 0, 2)
+        load_cand(1, 0, 2)
+        dc_product(1, 0)
+        load_incoming("i0b", 0, 256, 256)
+        load_grad_gate(1, 2, 2)
+        load_cand(1, 2, 2)
+        load_incoming("i0a", 0, 0, 256)
+        load_grad_gate(0, 2, 2)
+        gate_slope(1, 0)
+        dzi_product(1, 0)
+        transpose_pair(1, 0)
+        interleave("i0b", on_scalar)
+        load_cand(0, 2, 2)
+        load_incoming("i1", 1, 0, 512)
+        dc_product(1, 2)
+        copy_transposed(1, 0, 0, on_scalar)
+        gate_slope(1, 2)
+        dzi_product(1, 2)
+        load_grad_gate(0, 1, 1)
+        copy_transposed(1, 0, 1, on_scalar)
+        copy_transposed(1, 0, 2, on_scalar)
+        interleave_on_tensor("i0a")
+        dc_product(0, 2)
+        transpose_pair(1, 1)
+        copy_interleaved("i0a", 0, on_scalar)
+        interleave("t1", on_scalar)
+        load_grad_gate(0, 0, 1)
+        load_cand(0, 1, 1)
+        interleave_on_tensor("i1")
+        gate_slope(0, 2)
+        copy_transposed(1, 1, 2, on_scalar)
+        dzi_product(0, 2)
+        copy_transposed(1, 1, 1, on_scalar)
+        copy_transposed(1, 1, 0, on_scalar)
+        load_cand(0, 0, 1)
+        copy_interleaved("i1", 0, on_scalar)
+        transpose_pair(0, 1)
+        quantize("t1")
+        dc_product(0, 0)
+        dc_product(0, 1)
+        copy_interleaved("i1", 1, on_scalar)
+        copy_transposed(0, 1, 0, on_scalar)
+        gate_slope(0, 1)
+        gate_slope(0, 0)
+        dzi_product(0, 1)
+        copy_transposed(0, 1, 1, on_scalar)
+        dzi_product(0, 0)
+        transpose_pair(0, 0)
+        interleave("t0", on_vector)
+        quantize("i0b")
+        quantize("i1")
+        quantize("i0a")
+        out1_matmuls(6)
+        load_weight(0, 0)
+        copy_transposed(0, 1, 2, on_scalar)
+        interleave("w000", on_scalar)
+        copy_transposed(0, 0, 1, on_scalar)
+        out1_matmuls(4)
+        copy_transposed(0, 0, 0, on_scalar)
+        quantize("t0")
+        load_weight(0, 1)
+        interleave("w010", on_vector)
+        out1_matmuls(1)
+        load_weight(1, 0)
+        copy_transposed(0, 0, 2, on_scalar)
+        load_weight(1, 1)
+        out1_copy(6, 1, on_scalar)
+        out1_matmuls(3)
+        out1_copy(6, 0, on_scalar)
+        out1_copy(1, 0, on_scalar)
+        quantize("w000")
+        quantize("f01")
+        quantize("f00")
+        out1_copy(4, 1, on_scalar)
+        interleave("w100", on_vector)
+        out1_copy(4, 0, on_scalar)
+        out1_matmuls(5)
+        out1_copy(1, 1, on_scalar)
+        out1_copy(3, 1, on_vector)
+        out1_matmuls(0)
+        out1_copy(5, 0, on_vector)
+        quantize("f10")
+        out1_matmuls(2)
+        out1_copy(3, 0, on_scalar)
+        out1_copy(5, 1, on_scalar)
+        out1_copy(2, 0, on_scalar)
+        quantize("w010")
+        quantize("w100")
+        out1_copy(2, 1, on_scalar)
+        out0_pass(0, 0)
+        out0_pass(0, 1)
+        quantize("f11")
+        interleave("w110", on_vector)
+        out0_pass(0, 2)
+        quantize("w110")
+        interleave("w101", on_scalar)
+        interleave("w001", on_vector)
+        out1_copy(0, 0, on_scalar)
+        out0_pass(0, 3)
+        out1_copy(0, 1, on_scalar)
+        out0_copy(0, 0, on_scalar)
+        quantize("w001")
+        out0_copy(0, 1, on_scalar)
+        out1_matmuls(7)
+        out0_copy(0, 2, on_scalar)
+        out0_copy(0, 3, on_scalar)
+        interleave("w111", on_scalar)
+        quantize("w101")
+        out1_copy(7, 1, on_scalar)
+        interleave("w011", on_vector)
+        out0_pass(1, 0)
+        quantize("w011")
+        out1_copy(7, 0, on_vector)
+        quantize("w111")
+        out0_pass(1, 1)
+        out0_pass(1, 2)
+        out0_pass(1, 3)
+        out0_copy(1, 0, on_scalar)
+        out0_copy(1, 1, on_vector)
+        out0_copy(1, 2, on_scalar)
+        out0_copy(1, 3, on_vector)

@@ -257,122 +257,128 @@ def tile_lstmcell_pa_v_kernel(
         identity_bf16 = keep.tile([P, P], BF16, name="identb")
         make_identity(nc, identity_bf16[:])
 
-        load_grad_gate(1, 0, 2)
-        load_cand(1, 0, 2)
-        dc_product(1, 0)
+
+        load_grad_gate(0, 0, 2)
+        load_cand(0, 0, 2)
+        load_incoming("i1", 1, 0, 512)
+        load_grad_gate(0, 2, 2)
+        load_cand(0, 2, 2)
+        load_incoming("i0a", 0, 0, 256)
         load_incoming("i0b", 0, 256, 256)
         load_grad_gate(1, 2, 2)
         load_cand(1, 2, 2)
-        load_incoming("i0a", 0, 0, 256)
-        load_grad_gate(0, 2, 2)
-        gate_slope(1, 0)
-        dzi_product(1, 0)
-        transpose_pair(1, 0)
-        interleave("i0b", on_scalar)
-        load_cand(0, 2, 2)
-        load_incoming("i1", 1, 0, 512)
-        dc_product(1, 2)
-        copy_transposed(1, 0, 0, on_scalar)
-        gate_slope(1, 2)
-        dzi_product(1, 2)
-        load_grad_gate(0, 1, 1)
-        copy_transposed(1, 0, 1, on_scalar)
-        copy_transposed(1, 0, 2, on_scalar)
-        interleave_on_tensor("i0a")
-        dc_product(0, 2)
-        transpose_pair(1, 1)
-        copy_interleaved("i0a", 0, on_scalar)
-        interleave("t1", on_scalar)
-        load_grad_gate(0, 0, 1)
-        load_cand(0, 1, 1)
-        interleave_on_tensor("i1")
-        gate_slope(0, 2)
-        copy_transposed(1, 1, 2, on_scalar)
-        dzi_product(0, 2)
-        copy_transposed(1, 1, 1, on_scalar)
-        copy_transposed(1, 1, 0, on_scalar)
-        load_cand(0, 0, 1)
-        copy_interleaved("i1", 0, on_scalar)
-        transpose_pair(0, 1)
-        quantize("t1")
+        load_weight(0, 0)
+        load_grad_gate(1, 1, 1)
+        load_cand(1, 1, 1)
+        load_grad_gate(1, 0, 1)
+        load_cand(1, 0, 1)
+        load_weight(1, 0)
+        load_weight(0, 1)
+        load_weight(1, 1)
+
         dc_product(0, 0)
-        dc_product(0, 1)
-        copy_interleaved("i1", 1, on_scalar)
-        copy_transposed(0, 1, 0, on_scalar)
-        gate_slope(0, 1)
         gate_slope(0, 0)
-        dzi_product(0, 1)
-        copy_transposed(0, 1, 1, on_scalar)
         dzi_product(0, 0)
         transpose_pair(0, 0)
-        interleave("t0", on_vector)
-        quantize("i0b")
-        quantize("i1")
-        quantize("i0a")
-        out1_matmuls(6)
-        load_weight(0, 0)
-        copy_transposed(0, 1, 2, on_scalar)
-        interleave("w000", on_scalar)
-        copy_transposed(0, 0, 1, on_scalar)
-        out1_matmuls(4)
+        interleave("i1", on_scalar)
         copy_transposed(0, 0, 0, on_scalar)
-        quantize("t0")
-        load_weight(0, 1)
-        interleave("w010", on_vector)
-        out1_matmuls(1)
-        load_weight(1, 0)
+        interleave_on_tensor("i0a")
+        dc_product(0, 2)
+        copy_transposed(0, 0, 1, on_scalar)
+        gate_slope(0, 2)
+        quantize("i1")
         copy_transposed(0, 0, 2, on_scalar)
-        load_weight(1, 1)
-        out1_copy(6, 1, on_scalar)
-        out1_matmuls(3)
-        out1_copy(6, 0, on_scalar)
-        out1_copy(1, 0, on_scalar)
-        quantize("w000")
-        quantize("f01")
+        interleave("i0b", on_scalar)
+        dzi_product(0, 2)
+
+        dc_product(1, 2)
+        transpose_pair(0, 1)
+        gate_slope(1, 2)
         quantize("f00")
-        out1_copy(4, 1, on_scalar)
-        interleave("w100", on_vector)
-        out1_copy(4, 0, on_scalar)
-        out1_matmuls(5)
-        out1_copy(1, 1, on_scalar)
-        out1_copy(3, 1, on_vector)
+        copy_interleaved("i0a", 0, on_scalar)
+        interleave("t0", on_scalar)
+        copy_transposed(0, 1, 0, on_scalar)
+        dzi_product(1, 2)
+        copy_transposed(0, 1, 1, on_scalar)
+        copy_transposed(0, 1, 2, on_scalar)
+        transpose_pair(1, 1)
+        quantize("i0b")
+        interleave("w000", on_scalar)
+        quantize("t0")
+        gate_slope(1, 1)
+        quantize("i0a")
+        dc_product(1, 0)
+        gate_slope(1, 0)
+        copy_transposed(1, 1, 0, on_scalar)
+
         out1_matmuls(0)
-        out1_copy(5, 0, on_vector)
-        quantize("f10")
-        out1_matmuls(2)
-        out1_copy(3, 0, on_scalar)
-        out1_copy(5, 1, on_scalar)
-        out1_copy(2, 0, on_scalar)
-        quantize("w010")
-        quantize("w100")
-        out1_copy(2, 1, on_scalar)
-        out0_pass(0, 0)
-        out0_pass(0, 1)
-        quantize("f11")
-        interleave("w110", on_vector)
-        out0_pass(0, 2)
-        quantize("w110")
-        interleave("w101", on_scalar)
-        interleave("w001", on_vector)
+        out1_matmuls(1)
+        copy_transposed(1, 1, 1, on_scalar)
         out1_copy(0, 0, on_scalar)
-        out0_pass(0, 3)
+        dc_product(1, 1)
+        copy_transposed(1, 1, 2, on_scalar)
+        dzi_product(1, 0)
+        out1_matmuls(2)
         out1_copy(0, 1, on_scalar)
+        out1_copy(1, 0, on_scalar)
+        dzi_product(1, 1)
+        interleave("t1", on_vector)
+        transpose_pair(1, 0)
+        out1_copy(1, 1, on_scalar)
+        out1_copy(2, 0, on_scalar)
+        quantize("w000")
+        quantize("t1")
+        out1_copy(2, 1, on_scalar)
+        interleave("w100", on_vector)
+
+        out1_matmuls(4)
+        copy_transposed(1, 0, 0, on_scalar)
+        out1_matmuls(5)
+        copy_transposed(1, 0, 2, on_vector)
+        out1_matmuls(6)
+        copy_transposed(1, 0, 1, on_scalar)
+        out1_matmuls(7)
+        out1_copy(4, 1, on_scalar)
+        out1_copy(5, 0, on_scalar)
+        out1_copy(4, 0, on_vector)
+        out1_copy(5, 1, on_scalar)
+        out1_copy(6, 0, on_scalar)
+        out1_copy(6, 1, on_scalar)
+        quantize("f01")
+        quantize("f11")
+        interleave("w010", on_vector)
+
+        out0_pass(0, 0)
+        out1_copy(7, 0, on_scalar)
+        interleave("w001", on_scalar)
+        out1_copy(7, 1, on_scalar)
+        quantize("w100")
+        quantize("w010")
+        quantize("f10")
+        out0_pass(0, 1)
+        out0_pass(0, 2)
+        interleave("w110", on_vector)
+        quantize("w110")
+        out0_pass(0, 3)
+        interleave("w101", on_vector)
+
+        out1_matmuls(3)
         out0_copy(0, 0, on_scalar)
         quantize("w001")
-        out0_copy(0, 1, on_scalar)
-        out1_matmuls(7)
-        out0_copy(0, 2, on_scalar)
-        out0_copy(0, 3, on_scalar)
-        interleave("w111", on_scalar)
         quantize("w101")
-        out1_copy(7, 1, on_scalar)
         interleave("w011", on_vector)
-        out0_pass(1, 0)
+        out0_copy(0, 1, on_scalar)
         quantize("w011")
-        out1_copy(7, 0, on_vector)
-        quantize("w111")
+        out0_copy(0, 2, on_scalar)
+        interleave("w111", on_scalar)
+        out0_copy(0, 3, on_vector)
+
+        out0_pass(1, 0)
+        out1_copy(3, 0, on_scalar)
+        out1_copy(3, 1, on_scalar)
         out0_pass(1, 1)
         out0_pass(1, 2)
+        quantize("w111")
         out0_pass(1, 3)
         out0_copy(1, 0, on_scalar)
         out0_copy(1, 1, on_vector)

from contextlib import ExitStack

import concourse.mybir as mybir
from concourse.masks import make_identity

TOKENS, D_IN, D_H = 512, 1024, 1024
FLOPS = 2 * TOKENS * D_H * D_IN * 3
BYTES = (
    2 * TOKENS * D_IN + 2 * 2 * D_H * D_IN + 2 * 4 * TOKENS * D_H + 2 * TOKENS * D_H + 4 * TOKENS * D_IN + 4 * D_H * D_IN
)

F32 = mybir.dt.float32
BF16 = mybir.dt.bfloat16
U32 = mybir.dt.uint32
U8 = mybir.dt.uint8
E4M3 = mybir.dt.float8_e4m3fn_x4
E5M2 = mybir.dt.float8_e5m2_x4
MULT = mybir.AluOpType.mult
SUBTRACT = mybir.AluOpType.subtract

P = 128
PACK = 4
HALF = 512
BANKS = 8
STAGING = 8
OUT1_TILES = 5
OUT0_TILES = 4


def tile_lstmcell_pa_v_kernel(
    tc, incoming, h, W_i, b_W_i, W_c, b_W_c, U_i, b_U_i, U_c, b_U_c, I_gate, C_head, grad_out, out_0, out_1
):
    nc = tc.nc
    on_vector = nc.vector.tensor_copy
    on_scalar = nc.scalar.copy

    with ExitStack() as ctx:
        raw = ctx.enter_context(tc.tile_pool(name="raw", bufs=1))
        keep = ctx.enter_context(tc.tile_pool(name="keep", bufs=1))
        rot = ctx.enter_context(tc.tile_pool(name="rot", bufs=2))
        psum = ctx.enter_context(tc.psum_pool(name="psum", bufs=BANKS))
        ctx.enter_context(tc.manual_schedule())

        grad_view = grad_out.rearrange("(p j) w -> p j w", j=PACK)
        gate_view = I_gate.rearrange("(p j) w -> p j w", j=PACK)
        cand_view = C_head.rearrange("(p j) w -> p j w", j=PACK)
        incoming_view = incoming.rearrange("(p j) n -> p j n", j=PACK)
        weight_view = [
            W_i.rearrange("(g p j) n -> p g j n", g=2, j=PACK),
            W_c.rearrange("(g p j) n -> p g j n", g=2, j=PACK),
        ]
        out0_view = out_0.rearrange("(p j) n -> p j n", j=PACK)

        grad = {}
        gate = {}
        cand = {}
        slope = {}
        dc32 = {}
        dc32_slot = {}
        rows = {}
        grouped = {}
        place = {}
        codes = {}
        banks = {}
        transposed = {}
        staged = {}
        result = {}

        def load(view, shape, dtype, name):
            tile = raw.tile(shape, dtype, name=name)
            nc.sync.dma_start(out=tile[:], in_=view)
            return tile

        def new_codes(name):
            words = keep.tile([P, HALF], U32, name="c%s" % name, align_bytes=64)
            scales = keep.tile([P, HALF], U8, name="s%s" % name, align_bytes=64)
            codes[name] = (words, scales)

        def load_grad_gate(half, j0, slots):
            features = slice(HALF * half, HALF * (half + 1))
            unit = (half, j0)
            grad[unit] = load(grad_view[:, j0 : j0 + slots, features], [P, slots, HALF], BF16, "g%d%d" % unit)
            gate[unit] = load(gate_view[:, j0 : j0 + slots, features], [P, slots, HALF], F32, "ig%d%d" % unit)

        def load_cand(half, j0, slots):
            features = slice(HALF * half, HALF * (half + 1))
            cand[(half, j0)] = load(cand_view[:, j0 : j0 + slots, features], [P, slots, HALF], F32, "ch%d%d" % (half, j0))

        def load_incoming(name, n_half, first, columns):
            start = HALF * n_half + first
            rows[name] = load(incoming_view[:, :, start : start + columns], [P, PACK, columns], BF16, name)[:]
            if codes.get("i%d" % n_half) is None:
                new_codes("i%d" % n_half)
            place[name] = ("i%d" % n_half, first, columns)

        def load_weight(which, g):
            tile = load(weight_view[which][:, g, :, :], [P, PACK, D_IN], BF16, "w%d%d" % (which, g))
            for n_half in range(2):
                name = "w%d%d%d" % (which, g, n_half)
                rows[name] = tile[:, :, HALF * n_half : HALF * (n_half + 1)]
                new_codes(name)
                place[name] = (name, 0, HALF)

        dzi = [keep.tile([P, PACK, HALF], BF16, name="dzi%d" % half, align_bytes=64) for half in range(2)]
        for half in range(2):
            rows["t%d" % half] = dzi[half][:]
            new_codes("t%d" % half)
            place["t%d" % half] = ("t%d" % half, 0, HALF)

        def interleave(name, copy):
            tile = rot.tile([P, place[name][2], PACK], BF16, name="il", tag="il", bufs=STAGING, align_bytes=64)
            copy(
                out=tile[:].rearrange("p (c i) j -> p c j i", i=4),
                in_=rows[name].rearrange("p j (c i) -> p c j i", i=4),
            )
            grouped[name] = tile[:].rearrange("p n j -> p (n j)")

        def interleave_on_tensor(name):
            banks[name] = []
            for b in range(place[name][2] // (2 * P)):
                bank = psum.tile([P, 2 * P, PACK], BF16, name="bank", tag="bank")
                for part in range(2):
                    first = 2 * P * b + P * part
                    nc.tensor.matmul(
                        out=bank[:, P * part : P * (part + 1), :],
                        lhsT=identity_bf16[:],
                        rhs=rows[name][:, :, first : first + P].rearrange("p j n -> p n j"),
                        start=True,
                        stop=True,
                    )
                banks[name].append(bank)

        def copy_interleaved(name, b, copy):
            if staged.get(name) is None:
                staged[name] = rot.tile([P, place[name][2], PACK], BF16, name="il", tag="il", bufs=STAGING, align_bytes=64)
                grouped[name] = staged[name][:].rearrange("p n j -> p (n j)")
            copy(out=staged[name][:, 2 * P * b : 2 * P * (b + 1), :], in_=banks[name][b][:])

        def quantize(name):
            operand, first, columns = place[name]
            fmt = E4M3 if name[0] in "iw" else E5M2
            words, scales = codes[operand]
            nc.vector.quantize_mx(
                out=words[:, first : first + columns].bitcast(fmt),
                scales=scales[:, first : first + columns],
                in_=grouped[name],
            )

        def dc_product(half, j0):
            unit = (half, j0)
            dc32[unit] = keep.tile([P, grad[unit].shape[1], HALF], F32, name="dcf%d%d" % unit)
            nc.vector.tensor_tensor(out=dc32[unit][:], in0=grad[unit][:], in1=gate[unit][:], op=MULT)
            for jj in range(grad[unit].shape[1]):
                dc32_slot[(half, j0 + jj)] = dc32[unit][:, jj, :]

        def gate_slope(half, j0):
            unit = (half, j0)
            slope[unit] = rot.tile([P, grad[unit].shape[1], HALF], F32, name="v", tag="v", bufs=2)
            nc.vector.scalar_tensor_tensor(
                out=slope[unit][:], in0=gate[unit][:], scalar=1.0, in1=cand[unit][:], op0=SUBTRACT, op1=MULT
            )

        def dzi_product(half, j0):
            unit = (half, j0)
            nc.vector.scalar_tensor_tensor(
                out=dzi[half][:, j0 : j0 + grad[unit].shape[1], :],
                in0=slope[unit][:],
                scalar=-1.0,
                in1=dc32[unit][:],
                op0=MULT,
                op1=MULT,
            )

        def transpose_pair(half, pair):
            unit = (half, pair)
            dzi_bank = psum.tile([P, 2, 2, P], F32, name="bank", tag="bank")
            for jj in range(2):
                words = dzi[half][:, 2 * pair + jj, :].bitcast(F32)
                for u in range(2):
                    nc.tensor.transpose(dzi_bank[:, jj, u, :], words[:, u : HALF // 2 : 2], identity[:])
            banks[unit] = [dzi_bank]
            for jj in range(2):
                dc_bank = psum.tile([P, PACK, P], F32, name="bank", tag="bank")
                for t in range(PACK):
                    nc.tensor.transpose(dc_bank[:, t, :], dc32_slot[(half, 2 * pair + jj)][:, t:HALF:PACK], identity[:])
                banks[unit].append(dc_bank)
            transposed[unit] = keep.tile([P, 2, 2, P, PACK], BF16, name="fq%d%d" % unit, align_bytes=64)
            name = "f%d%d" % unit
            grouped[name] = transposed[unit][:].rearrange("p x j r t -> p (x j r t)")
            new_codes(name)
            place[name] = (name, 0, HALF)

        def copy_transposed(half, pair, bank, copy):
            unit = (half, pair)
            if bank == 0:
                copy(
                    out=transposed[unit][:, 0, :, :, :].bitcast(F32),
                    in_=banks[unit][0][:].rearrange("p j u r -> p j r u"),
                )
            else:
                copy(out=transposed[unit][:, 1, bank - 1, :, :], in_=banks[unit][bank][:].rearrange("p t r -> p r t"))

        def out1_matmuls(m):
            half, mm = divmod(m, 4)
            features = slice(P * mm, P * (mm + 1))
            dzi_words, dzi_scales = codes["t%d" % half]
            for n_half in range(2):
                bank = psum.tile([P, HALF], F32, name="bank", tag="bank")
                inc_words, inc_scales = codes["i%d" % n_half]
                nc.tensor.matmul_mx(
                    out=bank[:],
                    lhsT=dzi_words[:, features].bitcast(E5M2),
                    lhsT_scale=dzi_scales[:, features],
                    rhs=inc_words[:].bitcast(E4M3),
                    rhs_scale=inc_scales[:],
                    start=True,
                    stop=True,
                )
                banks[(1, m, n_half)] = bank

        def out1_copy(m, n_half, copy):
            if result.get(m) is None:
                result[m] = [rot.tile([P, D_IN], F32, name="o1", tag="o1", bufs=OUT1_TILES)]
            tile = result[m][0]
            copy(out=tile[:, HALF * n_half : HALF * (n_half + 1)], in_=banks[(1, m, n_half)][:])
            result[m].append(n_half)
            if len(result[m]) == 3:
                nc.sync.dma_start(out=out_1[P * m : P * (m + 1), :], in_=tile[:])

        passes = [(0, 0), (1, 0), (0, 1), (1, 1)]

        def out0_pass(n_half, s):
            which, g = passes[s]
            w_words, w_scales = codes["w%d%d%d" % (which, g, n_half)]
            for j in range(PACK):
                if s == 0:
                    banks[(0, j, n_half)] = psum.tile([P, HALF], F32, name="bank", tag="bank")
                dz_words, dz_scales = codes["f%d%d" % (g, j // 2)]
                first = (which * 2 + j % 2) * P
                nc.tensor.matmul_mx(
                    out=banks[(0, j, n_half)][:],
                    lhsT=dz_words[:, first : first + P].bitcast(E5M2),
                    lhsT_scale=dz_scales[:, first : first + P],
                    rhs=w_words[:].bitcast(E4M3),
                    rhs_scale=w_scales[:],
                    start=(s == 0),
                    stop=(s == len(passes) - 1),
                )

        def out0_copy(n_half, j, copy):
            tile = rot.tile([P, HALF], F32, name="o0", tag="o0", bufs=OUT0_TILES)
            copy(out=tile[:], in_=banks[(0, j, n_half)][:])
            nc.sync.dma_start(out=out0_view[:, j, HALF * n_half : HALF * (n_half + 1)], in_=tile[:])

        identity = keep.tile([P, P], F32, name="ident")
        make_identity(nc, identity[:])
        identity_bf16 = keep.tile([P, P], BF16, name="identb")
        make_identity(nc, identity_bf16[:])


        load_grad_gate(0, 0, 2)
        load_cand(0, 0, 2)
        load_incoming("i1", 1, 0, 512)
        load_grad_gate(0, 2, 2)
        load_cand(0, 2, 2)
        load_incoming("i0a", 0, 0, 256)
        load_incoming("i0b", 0, 256, 256)
        load_grad_gate(1, 2, 2)
        load_cand(1, 2, 2)
        load_weight(0, 0)
        load_grad_gate(1, 1, 1)
        load_cand(1, 1, 1)
        load_grad_gate(1, 0, 1)
        load_cand(1, 0, 1)
        load_weight(1, 0)
        load_weight(0, 1)
        load_weight(1, 1)

        dc_product(0, 0)
        gate_slope(0, 0)
        dzi_product(0, 0)
        transpose_pair(0, 0)
        interleave("i1", on_scalar)
        copy_transposed(0, 0, 0, on_scalar)
        interleave_on_tensor("i0a")
        dc_product(0, 2)
        copy_transposed(0, 0, 1, on_scalar)
        gate_slope(0, 2)
        quantize("i1")
        copy_transposed(0, 0, 2, on_scalar)
        interleave("i0b", on_scalar)
        dzi_product(0, 2)

        dc_product(1, 2)
        transpose_pair(0, 1)
        gate_slope(1, 2)
        quantize("f00")
        copy_interleaved("i0a", 0, on_scalar)
        interleave("t0", on_scalar)
        copy_transposed(0, 1, 0, on_scalar)
        dzi_product(1, 2)
        copy_transposed(0, 1, 1, on_scalar)
        copy_transposed(0, 1, 2, on_scalar)
        transpose_pair(1, 1)
        quantize("i0b")
        interleave("w000", on_scalar)
        quantize("t0")
        gate_slope(1, 1)
        quantize("i0a")
        dc_product(1, 0)
        gate_slope(1, 0)
        copy_transposed(1, 1, 0, on_scalar)

        out1_matmuls(0)
        out1_matmuls(1)
        copy_transposed(1, 1, 1, on_scalar)
        out1_copy(0, 0, on_scalar)
        dc_product(1, 1)
        copy_transposed(1, 1, 2, on_scalar)
        dzi_product(1, 0)
        out1_matmuls(2)
        out1_copy(0, 1, on_scalar)
        out1_copy(1, 0, on_scalar)
        dzi_product(1, 1)
        interleave("t1", on_vector)
        transpose_pair(1, 0)
        out1_copy(1, 1, on_scalar)
        out1_copy(2, 0, on_scalar)
        quantize("w000")
        quantize("t1")
        out1_copy(2, 1, on_scalar)
        interleave("w100", on_vector)

        out1_matmuls(4)
        copy_transposed(1, 0, 0, on_scalar)
        out1_matmuls(5)
        copy_transposed(1, 0, 2, on_vector)
        out1_matmuls(6)
        copy_transposed(1, 0, 1, on_scalar)
        out1_matmuls(7)
        out1_copy(4, 1, on_scalar)
        out1_copy(5, 0, on_scalar)
        out1_copy(4, 0, on_vector)
        out1_copy(5, 1, on_scalar)
        out1_copy(6, 0, on_scalar)
        out1_copy(6, 1, on_scalar)
        quantize("f01")
        quantize("f11")
        interleave("w010", on_vector)

        out0_pass(0, 0)
        out1_copy(7, 0, on_scalar)
        interleave("w001", on_scalar)
        out1_copy(7, 1, on_scalar)
        quantize("w100")
        quantize("w010")
        quantize("f10")
        out0_pass(0, 1)
        out0_pass(0, 2)
        interleave("w110", on_vector)
        quantize("w110")
        out0_pass(0, 3)
        interleave("w101", on_vector)

        out1_matmuls(3)
        out0_copy(0, 0, on_scalar)
        quantize("w001")
        quantize("w101")
        interleave("w011", on_vector)
        out0_copy(0, 1, on_scalar)
        quantize("w011")
        out0_copy(0, 2, on_scalar)
        interleave("w111", on_scalar)
        out0_copy(0, 3, on_vector)

        out0_pass(1, 0)
        out1_copy(3, 0, on_scalar)
        out1_copy(3, 1, on_scalar)
        out0_pass(1, 1)
        out0_pass(1, 2)
        quantize("w111")
        out0_pass(1, 3)
        out0_copy(1, 0, on_scalar)
        out0_copy(1, 1, on_vector)
        out0_copy(1, 2, on_scalar)
        out0_copy(1, 3, on_vector)
